import numpy as np
import ml_dtypes


def mxq(x, axis, fmt="e4m3"):
    dtype, down = {"e4m3": (ml_dtypes.float8_e4m3fn, 7), "e5m2": (ml_dtypes.float8_e5m2, 14)}[fmt]
    v = np.moveaxis(np.asarray(x, np.float32).astype(ml_dtypes.bfloat16).astype(np.float64), axis, -1)
    blocks = v.reshape(v.shape[:-1] + (-1, 32))
    amax = np.abs(blocks).max(-1, keepdims=True)
    byte = np.maximum(np.where(amax > 0, np.frexp(amax)[1] - 1 + 127, 0) - down, 1)
    scale = np.exp2(byte - 127.0)
    codes = (blocks / scale).astype(np.float32).astype(dtype).astype(np.float64)
    return np.moveaxis((codes * scale).reshape(v.shape), -1, axis)


WIDE = False


def mx_kscale(k):
    if not WIDE:
        return np.ones(k)
    levels = np.array([10, -10, 5, -5, 0])
    a = np.random.permutation(np.resize(levels, k // 512 * 4)).reshape(k // 512, 4)
    idx = np.arange(k)
    return np.exp2(a[idx // 512, idx % 128 // 32])


BF16 = ml_dtypes.bfloat16


def bf(x):
    return np.asarray(x, np.float32).astype(BF16)


def f64(x):
    return np.asarray(x).astype(np.float64)


E2M1 = np.array([0.0, 0.5, 1.0, 1.5, 2.0, 3.0, 4.0, 6.0, -0.0, -0.5, -1.0, -1.5, -2.0, -3.0, -4.0, -6.0])


def pack_weight(w, fmt):
    k, n = w.shape
    w = f64(bf(w)).reshape(k // 32, 32, n)
    amax = np.abs(w).max(1)
    if fmt == "e4m3":
        byte = np.frexp(amax)[1] - 1 + 127 - 7
    else:
        mant, ex = np.frexp(amax / 6.0)
        byte = np.where(mant > 0.5, ex, ex - 1) + 127
    byte = np.clip(np.where(amax > 0, byte, 1), 1, 254)
    scaled = (w * np.exp2(127.0 - byte)[:, None, :]).reshape(k, n).astype(np.float32)
    by_word = np.ascontiguousarray(scaled.reshape(k // 512, 128, 4, n).transpose(0, 1, 3, 2))
    if fmt == "e4m3":
        words = by_word.astype(ml_dtypes.float8_e4m3fn).view(np.uint8)
    else:
        c = by_word.astype(ml_dtypes.float4_e2m1fn).view(np.uint8) & 0xF
        words = c[..., 0::2] | (c[..., 1::2] << 4)
    return np.ascontiguousarray(words), np.ascontiguousarray(byte.astype(np.uint8).reshape(k // 512, 16, n))


def unpack_weight(words, scales, fmt):
    g, p, n, _ = words.shape
    if fmt == "e4m3":
        vals = np.ascontiguousarray(words).view(ml_dtypes.float8_e4m3fn).astype(np.float64)
    else:
        nib = np.empty((g, p, n, 4), np.uint8)
        nib[..., 0::2] = words & 0xF
        nib[..., 1::2] = words >> 4
        vals = E2M1[nib]
    vals = vals * np.repeat(np.exp2(scales.astype(np.float64) - 127.0), 8, axis=1)[..., None]
    return vals.transpose(0, 1, 3, 2).reshape(g * 512, n)


B, N, E, H, NOPE, VDIM, ROPE, QR, KVR = 4, 256, 2048, 16, 128, 128, 128, 512, 512
QH = NOPE + ROPE
BASE = 10000.0
FMT = "e4m3"


def rope(v):
    d = v.shape[-1]
    n = v.shape[-2]
    theta = BASE ** (-2.0 * np.arange(d // 2) / d)
    ang = np.arange(n)[:, None] * theta[None, :]
    cos, sin = np.cos(ang), np.sin(ang)
    v1, v2 = v[..., 0::2], v[..., 1::2]
    return np.stack([v1 * cos - v2 * sin, v1 * sin + v2 * cos], axis=-1).reshape(v.shape)


def setup_inputs():
    s, t = mx_kscale(E), mx_kscale(QR)
    x = bf(np.random.standard_normal((B, N, E)) * s)
    Wqa_words, Wqa_scales = pack_weight(np.random.standard_normal((E, QR)) / np.sqrt(E) / s[:, None] * t, FMT)
    Wqb_words, Wqb_scales = pack_weight(np.random.standard_normal((QR, H * QH)) / np.sqrt(QR) / t[:, None], FMT)
    return {"x": x,
            "Wqa_words": Wqa_words, "Wqa_scales": Wqa_scales,
            "Wqb_words": Wqb_words, "Wqb_scales": Wqb_scales}


def reference(x, Wqa_words, Wqa_scales, Wqb_words, Wqb_scales):
    cq = mxq(f64(x), 2, "e4m3") @ unpack_weight(Wqa_words, Wqa_scales, FMT)
    q = mxq(cq, 2, "e4m3") @ unpack_weight(Wqb_words, Wqb_scales, FMT)
    q = q.reshape(B, N, H, QH).transpose(0, 2, 1, 3)
    return np.concatenate([q[..., :NOPE], rope(q[..., NOPE:])], axis=-1)

@@ -1,0 +1,271 @@
+import math
+from contextlib import ExitStack
+
+import concourse.mybir as mybir
+from concourse.masks import make_identity
+
+F32 = mybir.dt.float32
+BF16 = mybir.dt.bfloat16
+I32 = mybir.dt.int32
+U32 = mybir.dt.uint32
+U8 = mybir.dt.uint8
+FP8X4 = mybir.dt.float8_e4m3fn_x4
+ALU = mybir.AluOpType
+ACT = mybir.ActivationFunctionType
+
+P = 128
+PACK = 4
+K_PASS = P * PACK
+
+BATCH, POSITIONS, FEATURES = 4, 256, 2048
+RANK = 512
+HEADS, NOPE, ROPE = 16, 128, 128
+HEAD = NOPE + ROPE
+PAIRS = ROPE // 2
+BASE = 10000.0
+
+HALVES = POSITIONS // P
+X_PASSES = FEATURES // K_PASS
+GROUP = 4
+GROUPS = HEADS // GROUP
+GROUP_COLS = GROUP * HEAD
+
+FLOPS = 2 * BATCH * POSITIONS * (FEATURES * RANK + RANK * HEADS * HEAD)
+
+
+def build_rotation_tables(nc, pool):
+    ratio = BASE ** (-2.0 / ROPE)
+    frequency = pool.tile([P, PAIRS], F32, name="frequency")
+    nc.vector.memset(frequency[:, 0:1], 1.0)
+    width = 1
+    while width < PAIRS:
+        nc.vector.tensor_scalar_mul(
+            out=frequency[:, width : 2 * width], in0=frequency[:, 0:width], scalar1=ratio**width
+        )
+        width *= 2
+
+    position_int = pool.tile([P, HALVES], I32, name="position_int")
+    nc.gpsimd.iota(position_int[:], pattern=[[1, HALVES]], base=0, channel_multiplier=HALVES)
+    position = pool.tile([P, HALVES], F32, name="position")
+    nc.vector.tensor_copy(out=position[:], in_=position_int[:])
+
+    turns = pool.tile([P, HALVES, PAIRS], F32, name="turns")
+    for s in range(HALVES):
+        nc.vector.tensor_scalar(
+            out=turns[:, s, :],
+            in0=frequency[:],
+            scalar1=position[:, s : s + 1],
+            scalar2=1.0 / (2.0 * math.pi),
+            op0=ALU.mult,
+            op1=ALU.mult,
+        )
+
+    whole_int = pool.tile([P, HALVES, PAIRS], I32, name="whole_int")
+    nc.vector.tensor_copy(out=whole_int[:], in_=turns[:])
+    whole = pool.tile([P, HALVES, PAIRS], F32, name="whole")
+    nc.vector.tensor_copy(out=whole[:], in_=whole_int[:])
+    part = pool.tile([P, HALVES, PAIRS], F32, name="part")
+    nc.vector.tensor_sub(out=part[:], in0=turns[:], in1=whole[:])
+    part_cos = pool.tile([P, HALVES, PAIRS], F32, name="part_cos")
+    nc.vector.tensor_scalar_add(out=part_cos[:], in0=part[:], scalar1=0.25)
+
+    minus_sin_turns = pool.tile([P, HALVES, PAIRS], F32, name="minus_sin_turns")
+    nc.vector.scalar_tensor_tensor(
+        out=minus_sin_turns[:], in0=part[:], scalar=0.5, in1=part[:], op0=ALU.is_gt, op1=ALU.subtract
+    )
+    minus_cos_turns = pool.tile([P, HALVES, PAIRS], F32, name="minus_cos_turns")
+    nc.vector.scalar_tensor_tensor(
+        out=minus_cos_turns[:], in0=part_cos[:], scalar=0.5, in1=part_cos[:], op0=ALU.is_gt, op1=ALU.subtract
+    )
+
+    sin_pairs = pool.tile([P, HALVES, PAIRS, 2], F32, name="sin_pairs")
+    nc.scalar.activation(out=sin_pairs[:, :, :, 0], in_=minus_sin_turns[:], func=ACT.Sin, scale=2.0 * math.pi)
+    nc.scalar.activation(out=sin_pairs[:, :, :, 1], in_=minus_sin_turns[:], func=ACT.Sin, scale=-2.0 * math.pi)
+    cos_pairs = pool.tile([P, HALVES, PAIRS, 2], F32, name="cos_pairs")
+    nc.scalar.activation(
+        out=cos_pairs[:],
+        in_=minus_cos_turns[:].unsqueeze(3).to_broadcast([P, HALVES, PAIRS, 2]),
+        func=ACT.Sin,
+        scale=-2.0 * math.pi,
+    )
+    return cos_pairs, sin_pairs
+
+
+def tile_multilatentattention_pa_kernel(tc, x, Wqa_words, Wqa_scales, Wqb_words, Wqb_scales, out):
+    nc = tc.nc
+    with ExitStack() as ctx:
+        keep = ctx.enter_context(tc.tile_pool(name="keep", bufs=1))
+        work = ctx.enter_context(tc.tile_pool(name="work", bufs=2))
+        swap = ctx.enter_context(tc.tile_pool(name="swap", bufs=4))
+        results = ctx.enter_context(tc.tile_pool(name="results", bufs=6))
+        psum = ctx.enter_context(tc.psum_pool(name="psum", bufs=1))
+
+        wqa_planes = keep.tile([P, RANK], U8, name="wqa_planes", align_bytes=64)
+        wqb_planes = keep.tile([P, GROUP_COLS], U8, name="wqb_planes", align_bytes=64)
+        nc.vector.memset(wqa_planes[:].bitcast(I32), 0)
+        nc.vector.memset(wqb_planes[:].bitcast(I32), 0)
+
+        x_sb = [keep.tile([P, HALVES * FEATURES], BF16, name="x%d" % b) for b in range(BATCH)]
+        wqa_w = keep.tile([P, X_PASSES, RANK], U32, name="wqa_w", align_bytes=64)
+        wqb_w = keep.tile([P, HEADS * HEAD], U32, name="wqb_w", align_bytes=64)
+        wqb_dram = Wqb_words.rearrange("g p n t -> p (g n t)").bitcast(I32)
+
+        def load_x(b):
+            nc.sync.dma_start(out=x_sb[b][:], in_=x[b].rearrange("(p s) e -> p (s e)", s=HALVES))
+
+        def load_planes(planes, scale_rows):
+            for quadrant in range(4):
+                nc.sync.dma_start(
+                    out=planes[32 * quadrant : 32 * quadrant + 16, :].bitcast(I32),
+                    in_=scale_rows[:, 4 * quadrant : 4 * quadrant + 4, :].bitcast(I32),
+                )
+
+        def load_wqb(k):
+            cols = slice(GROUP_COLS * k, GROUP_COLS * (k + 1))
+            nc.sync.dma_start(out=wqb_w[:, cols].bitcast(I32), in_=wqb_dram[:, cols])
+
+        load_x(0)
+        load_planes(wqa_planes, Wqa_scales)
+        nc.sync.dma_start(
+            out=wqa_w[:].bitcast(I32), in_=Wqa_words.rearrange("g p n t -> p g (n t)").bitcast(I32)
+        )
+        load_planes(wqb_planes, Wqb_scales[0].rearrange("r (k c) -> k r c", k=GROUPS))
+        load_wqb(0)
+        load_x(1)
+        for k in range(1, GROUPS):
+            load_wqb(k)
+        load_x(2)
+        load_x(3)
+
+        ident_f32 = keep.tile([P, P], F32, name="ident_f32")
+        make_identity(nc, ident_f32[:])
+        ident_bf16 = keep.tile([P, P], BF16, name="ident_bf16")
+        make_identity(nc, ident_bf16[:])
+        cos_pairs, sin_pairs = build_rotation_tables(nc, keep)
+
+        cq_codes = [keep.tile([P, HALVES, P], U32, name="cq_codes%d" % b, align_bytes=64) for b in range(BATCH)]
+        cq_scales = [keep.tile([P, HALVES, P], U8, name="cq_scales%d" % b, align_bytes=64) for b in range(BATCH)]
+
+        x_grouped, x_codes, x_scales, cq_sorted, cq_grouped = {}, {}, {}, {}, {}
+
+        def transpose_x(b, s):
+            x_pairs = x_sb[b][:].bitcast(F32)
+            x_grouped[b, s] = work.tile([P, FEATURES], BF16, name="x_grouped", align_bytes=64)
+            grouped_pairs = x_grouped[b, s][:].bitcast(F32).rearrange("p (g r u) -> p g r u", g=X_PASSES, u=2)
+            for half in range(2):
+                x_t = psum.tile([P, 2, 2, P], F32, name="x_t", bufs=2)
+                for i in range(2):
+                    first = (FEATURES // 2) * s + (K_PASS // 2) * (2 * half + i)
+                    for u in range(2):
+                        nc.tensor.transpose(
+                            x_t[:, i, u, :], x_pairs[:, first + u : first + K_PASS // 2 : 2], ident_f32[:]
+                        )
+                nc.scalar.copy(
+                    out=grouped_pairs[:, 2 * half : 2 * half + 2], in_=x_t[:].rearrange("p g u r -> p g r u")
+                )
+
+        def quantise_x(b, s):
+            x_codes[b, s] = work.tile([P, X_PASSES, P], U32, name="x_codes", align_bytes=64)
+            x_scales[b, s] = work.tile([P, X_PASSES, P], U8, name="x_scales", align_bytes=64)
+            nc.vector.quantize_mx(
+                out=x_codes[b, s][:].rearrange("p g r -> p (g r)").bitcast(FP8X4),
+                scales=x_scales[b, s][:].rearrange("p g r -> p (g r)"),
+                in_=x_grouped[b, s][:],
+            )
+
+        def contract_x(b, s):
+            cq_sum = psum.tile([P, RANK], F32, name="cq_sum", tag="cq")
+            for g in range(X_PASSES):
+                nc.tensor.matmul_mx(
+                    out=cq_sum[:],
+                    lhsT=x_codes[b, s][:, g, :].bitcast(FP8X4),
+                    lhsT_scale=x_scales[b, s][:, g, :],
+                    rhs=wqa_w[:, g, :].bitcast(FP8X4),
+                    rhs_scale=wqa_planes[4 * g : P, :],
+                    start=(g == 0),
+                    stop=(g == X_PASSES - 1),
+                )
+            if s == 0:
+                cq_sorted[b] = work.tile([P, HALVES, PACK, P], BF16, name="cq_sorted")
+            nc.scalar.copy(out=cq_sorted[b][:, s], in_=cq_sum[:].rearrange("r (p t) -> r t p", t=PACK))
+
+        def transpose_cq(b):
+            cq_t = psum.tile([P, HALVES, PACK, P], BF16, name="cq_t", tag="cq")
+            for s in range(HALVES):
+                for t in range(PACK):
+                    nc.tensor.transpose(cq_t[:, s, t, :], cq_sorted[b][:, s, t, :], ident_bf16[:])
+            cq_grouped[b] = work.tile([P, HALVES, P, PACK], BF16, name="cq_grouped", align_bytes=64)
+            nc.scalar.copy(out=cq_grouped[b][:], in_=cq_t[:].rearrange("p s t r -> p s r t"))
+
+        def quantise_cq(b):
+            nc.vector.quantize_mx(
+                out=cq_codes[b][:].rearrange("p s r -> p (s r)").bitcast(FP8X4),
+                scales=cq_scales[b][:].rearrange("p s r -> p (s r)"),
+                in_=cq_grouped[b][:].rearrange("p s r t -> p (s r t)"),
+            )
+
+        def project_up_and_rotate(b, k):
+            result = results.tile([P, GROUP, HALVES, HEAD], F32, name="result")
+            crossed = swap.tile([P, GROUP, HALVES, ROPE], F32, name="crossed")
+            for s in range(HALVES):
+                rope = psum.tile([P, GROUP, ROPE], F32, name="rope", bufs=3)
+                nope = psum.tile([P, GROUP, NOPE], F32, name="nope", bufs=2)
+                for bank, offset in ((rope, NOPE), (nope, 0)):
+                    for j in range(GROUP):
+                        col = HEAD * j + offset
+                        nc.tensor.matmul_mx(
+                            out=bank[:, j, :],
+                            lhsT=cq_codes[b][:, s, :].bitcast(FP8X4),
+                            lhsT_scale=cq_scales[b][:, s, :],
+                            rhs=wqb_w[:, GROUP_COLS * k + col : GROUP_COLS * k + col + P].bitcast(FP8X4),
+                            rhs_scale=wqb_planes[4 * k : P, col : col + P],
+                            start=True,
+                            stop=True,
+                        )
+                nc.scalar.copy(out=result[:, :, s, 0:NOPE], in_=nope[:])
+
+                nc.vector.tensor_tensor(
+                    out=result[:, :, s, NOPE:HEAD],
+                    in0=rope[:],
+                    in1=cos_pairs[:, s].rearrange("p i e -> p (i e)").unsqueeze(1).to_broadcast([P, GROUP, ROPE]),
+                    op=ALU.mult,
+                )
+                nc.vector.tensor_tensor(
+                    out=crossed[:, :, s, :].rearrange("p h (i e) -> p h i e", e=2),
+                    in0=rope[:].rearrange("p h (i e) -> p h i e", e=2)[:, :, :, ::-1],
+                    in1=sin_pairs[:, s].unsqueeze(1).to_broadcast([P, GROUP, PAIRS, 2]),
+                    op=ALU.mult,
+                )
+            nc.gpsimd.tensor_tensor(
+                out=result[:, :, :, NOPE:HEAD], in0=result[:, :, :, NOPE:HEAD], in1=crossed[:], op=ALU.add
+            )
+            nc.sync.dma_start(
+                out=out[b, GROUP * k : GROUP * (k + 1)].rearrange("h (p s) f -> p h (s f)", s=HALVES),
+                in_=result[:].rearrange("p h s f -> p h (s f)"),
+            )
+
+        transpose_x(0, 0)
+        quantise_x(0, 0)
+        transpose_x(0, 1)
+        contract_x(0, 0)
+        quantise_x(0, 1)
+        contract_x(0, 1)
+        transpose_cq(0)
+        quantise_cq(0)
+        for b in range(BATCH):
+            ahead = b + 1 < BATCH
+            project_up_and_rotate(b, 0)
+            if ahead:
+                transpose_x(b + 1, 0)
+                quantise_x(b + 1, 0)
+            project_up_and_rotate(b, 1)
+            if ahead:
+                contract_x(b + 1, 0)
+                transpose_x(b + 1, 1)
+                quantise_x(b + 1, 1)
+            project_up_and_rotate(b, 2)
+            if ahead:
+                contract_x(b + 1, 1)
+                transpose_cq(b + 1)
+                quantise_cq(b + 1)
+            project_up_and_rotate(b, 3)

@@ -236,9 +236,9 @@ def tile_multilatentattention_pa_kernel(tc, x, Wqa_words, Wqa_scales, Wqb_words,
                     in1=sin_pairs[:, s].unsqueeze(1).to_broadcast([P, GROUP, PAIRS, 2]),
                     op=ALU.mult,
                 )
-            nc.gpsimd.tensor_tensor(
-                out=result[:, :, :, NOPE:HEAD], in0=result[:, :, :, NOPE:HEAD], in1=crossed[:], op=ALU.add
-            )
+                nc.gpsimd.tensor_tensor(
+                    out=result[:, :, s, NOPE:HEAD], in0=result[:, :, s, NOPE:HEAD], in1=crossed[:, :, s, :], op=ALU.add
+                )
             nc.sync.dma_start(
                 out=out[b, GROUP * k : GROUP * (k + 1)].rearrange("h (p s) f -> p h (s f)", s=HALVES),
                 in_=result[:].rearrange("p h s f -> p h (s f)"),

@@ -33,6 +33,10 @@ GROUP_COLS = GROUP * HEAD
 FLOPS = 2 * BATCH * POSITIONS * (FEATURES * RANK + RANK * HEADS * HEAD)
 
 
+T_AT0 = (1, 2, 5, 5, 6, 7)
+T_AT = (0, 1, 4, 4, 5, 7)
+
+
 def build_rotation_tables(nc, pool):
     ratio = BASE ** (-2.0 / ROPE)
     frequency = pool.tile([P, PAIRS], F32, name="frequency")
@@ -100,18 +104,22 @@ def tile_multilatentattention_pa_kernel(tc, x, Wqa_words, Wqa_scales, Wqb_words,
         results = ctx.enter_context(tc.tile_pool(name="results", bufs=6))
         psum = ctx.enter_context(tc.psum_pool(name="psum", bufs=1))
 
+        wqa_planes_raw = keep.tile([P, RANK], U8, name="wqa_planes_raw", align_bytes=64)
         wqa_planes = keep.tile([P, RANK], U8, name="wqa_planes", align_bytes=64)
         wqb_planes = keep.tile([P, GROUP_COLS], U8, name="wqb_planes", align_bytes=64)
-        nc.vector.memset(wqa_planes[:].bitcast(I32), 0)
+        nc.vector.memset(wqa_planes_raw[:].bitcast(I32), 0)
         nc.vector.memset(wqb_planes[:].bitcast(I32), 0)
 
-        x_sb = [keep.tile([P, HALVES * FEATURES], BF16, name="x%d" % b) for b in range(BATCH)]
-        wqa_w = keep.tile([P, X_PASSES, RANK], U32, name="wqa_w", align_bytes=64)
+        x_sb = [keep.tile([P, HALVES, FEATURES], BF16, name="x%d" % b) for b in range(BATCH)]
+        wqa_raw = keep.tile([P, X_PASSES, RANK], I32, name="wqa_raw", align_bytes=64)
+        wqa_w = keep.tile([P, X_PASSES, PACK, P], I32, name="wqa_w", align_bytes=64)
         wqb_w = keep.tile([P, HEADS * HEAD], U32, name="wqb_w", align_bytes=64)
         wqb_dram = Wqb_words.rearrange("g p n t -> p (g n t)").bitcast(I32)
 
-        def load_x(b):
-            nc.sync.dma_start(out=x_sb[b][:], in_=x[b].rearrange("(p s) e -> p (s e)", s=HALVES))
+        def load_x(b, halves):
+            nc.sync.dma_start(
+                out=x_sb[b][:, halves, :], in_=x[b].rearrange("(p s) e -> p s e", s=HALVES)[:, halves, :]
+            )
 
         def load_planes(planes, scale_rows):
             for quadrant in range(4):
@@ -120,152 +128,172 @@ def tile_multilatentattention_pa_kernel(tc, x, Wqa_words, Wqa_scales, Wqb_words,
                     in_=scale_rows[:, 4 * quadrant : 4 * quadrant + 4, :].bitcast(I32),
                 )
 
+        def load_wqa(passes):
+            nc.sync.dma_start(
+                out=wqa_raw[:, passes, :], in_=Wqa_words.rearrange("g p n t -> p g (n t)").bitcast(I32)[:, passes, :]
+            )
+
         def load_wqb(k):
             cols = slice(GROUP_COLS * k, GROUP_COLS * (k + 1))
             nc.sync.dma_start(out=wqb_w[:, cols].bitcast(I32), in_=wqb_dram[:, cols])
 
-        load_x(0)
-        load_planes(wqa_planes, Wqa_scales)
-        nc.sync.dma_start(
-            out=wqa_w[:].bitcast(I32), in_=Wqa_words.rearrange("g p n t -> p g (n t)").bitcast(I32)
-        )
+        load_x(0, slice(0, 1))
+        load_planes(wqa_planes_raw, Wqa_scales)
+        load_wqa(slice(0, 2))
+        load_wqa(slice(2, 4))
+        load_x(0, slice(1, 2))
         load_planes(wqb_planes, Wqb_scales[0].rearrange("r (k c) -> k r c", k=GROUPS))
         load_wqb(0)
-        load_x(1)
-        for k in range(1, GROUPS):
-            load_wqb(k)
-        load_x(2)
-        load_x(3)
+        load_wqb(1)
+        load_x(1, slice(0, 2))
+        load_wqb(2)
+        load_wqb(3)
+        load_x(2, slice(0, 2))
+        load_x(3, slice(0, 2))
 
         ident_f32 = keep.tile([P, P], F32, name="ident_f32")
         make_identity(nc, ident_f32[:])
-        ident_bf16 = keep.tile([P, P], BF16, name="ident_bf16")
-        make_identity(nc, ident_bf16[:])
         cos_pairs, sin_pairs = build_rotation_tables(nc, keep)
 
+        nc.gpsimd.tensor_copy(
+            out=wqa_planes[:].rearrange("p (t m) -> p m t", t=PACK),
+            in_=wqa_planes_raw[:].rearrange("p (m t) -> p m t", t=PACK),
+        )
+        for g in range(X_PASSES):
+            nc.vector.tensor_copy(out=wqa_w[:, g], in_=wqa_raw[:, g, :].rearrange("p (m t) -> p t m", t=PACK))
+
+        x_grouped = [None] * BATCH
+        x_codes = [None] * BATCH
+        x_scales = [None] * BATCH
+        cq_grouped = [None] * BATCH
         cq_codes = [keep.tile([P, HALVES, P], U32, name="cq_codes%d" % b, align_bytes=64) for b in range(BATCH)]
         cq_scales = [keep.tile([P, HALVES, P], U8, name="cq_scales%d" % b, align_bytes=64) for b in range(BATCH)]
 
-        x_grouped, x_codes, x_scales, cq_sorted, cq_grouped = {}, {}, {}, {}, {}
-
-        def transpose_x(b, s):
-            x_pairs = x_sb[b][:].bitcast(F32)
-            x_grouped[b, s] = work.tile([P, FEATURES], BF16, name="x_grouped", align_bytes=64)
-            grouped_pairs = x_grouped[b, s][:].bitcast(F32).rearrange("p (g r u) -> p g r u", g=X_PASSES, u=2)
+        def transpose_x(b, s, helper):
+            x_pairs = x_sb[b][:, s, :].bitcast(F32)
+            if s == 0:
+                x_grouped[b] = work.tile([P, HALVES, FEATURES], BF16, name="x_grouped", align_bytes=64)
+            grouped_pairs = x_grouped[b][:, s, :].bitcast(F32).rearrange("p (g r u) -> p g r u", g=X_PASSES, u=2)
             for half in range(2):
                 x_t = psum.tile([P, 2, 2, P], F32, name="x_t", bufs=2)
                 for i in range(2):
-                    first = (FEATURES // 2) * s + (K_PASS // 2) * (2 * half + i)
+                    first = (K_PASS // 2) * (2 * half + i)
                     for u in range(2):
                         nc.tensor.transpose(
                             x_t[:, i, u, :], x_pairs[:, first + u : first + K_PASS // 2 : 2], ident_f32[:]
                         )
-                nc.scalar.copy(
-                    out=grouped_pairs[:, 2 * half : 2 * half + 2], in_=x_t[:].rearrange("p g u r -> p g r u")
-                )
+                copy = nc.vector.tensor_copy if (helper and half == 1) else nc.scalar.copy
+                copy(out=grouped_pairs[:, 2 * half : 2 * half + 2], in_=x_t[:].rearrange("p g u r -> p g r u"))
 
-        def quantise_x(b, s):
-            x_codes[b, s] = work.tile([P, X_PASSES, P], U32, name="x_codes", align_bytes=64)
-            x_scales[b, s] = work.tile([P, X_PASSES, P], U8, name="x_scales", align_bytes=64)
+        def quantise_x(b, halves):
+            if halves.start == 0:
+                x_codes[b] = work.tile([P, HALVES, X_PASSES, P], U32, name="x_codes", align_bytes=64)
+                x_scales[b] = work.tile([P, HALVES, X_PASSES, P], U8, name="x_scales", align_bytes=64)
             nc.vector.quantize_mx(
-                out=x_codes[b, s][:].rearrange("p g r -> p (g r)").bitcast(FP8X4),
-                scales=x_scales[b, s][:].rearrange("p g r -> p (g r)"),
-                in_=x_grouped[b, s][:],
+                out=x_codes[b][:, halves].rearrange("p s g r -> p (s g r)").bitcast(FP8X4),
+                scales=x_scales[b][:, halves].rearrange("p s g r -> p (s g r)"),
+                in_=x_grouped[b][:, halves].rearrange("p s e -> p (s e)"),
             )
 
         def contract_x(b, s):
-            cq_sum = psum.tile([P, RANK], F32, name="cq_sum", tag="cq")
-            for g in range(X_PASSES):
-                nc.tensor.matmul_mx(
-                    out=cq_sum[:],
-                    lhsT=x_codes[b, s][:, g, :].bitcast(FP8X4),
-                    lhsT_scale=x_scales[b, s][:, g, :],
-                    rhs=wqa_w[:, g, :].bitcast(FP8X4),
-                    rhs_scale=wqa_planes[4 * g : P, :],
-                    start=(g == 0),
-                    stop=(g == X_PASSES - 1),
-                )
+            cq_t = psum.tile([P, PACK, P], F32, name="cq_t", tag="cq")
+            for t in range(PACK):
+                for g in range(X_PASSES):
+                    nc.tensor.matmul_mx(
+                        out=cq_t[:, t, :],
+                        lhsT=wqa_w[:, g, t, :].bitcast(FP8X4),
+                        lhsT_scale=wqa_planes[4 * g : P, P * t : P * (t + 1)],
+                        rhs=x_codes[b][:, s, g, :].bitcast(FP8X4),
+                        rhs_scale=x_scales[b][:, s, g, :],
+                        start=(g == 0),
+                        stop=(g == X_PASSES - 1),
+                    )
             if s == 0:
-                cq_sorted[b] = work.tile([P, HALVES, PACK, P], BF16, name="cq_sorted")
-            nc.scalar.copy(out=cq_sorted[b][:, s], in_=cq_sum[:].rearrange("r (p t) -> r t p", t=PACK))
+                cq_grouped[b] = work.tile([P, HALVES, P, PACK], BF16, name="cq_grouped", align_bytes=64)
+            nc.scalar.copy(out=cq_grouped[b][:, s], in_=cq_t[:].rearrange("p t r -> p r t"))
 
-        def transpose_cq(b):
-            cq_t = psum.tile([P, HALVES, PACK, P], BF16, name="cq_t", tag="cq")
-            for s in range(HALVES):
-                for t in range(PACK):
-                    nc.tensor.transpose(cq_t[:, s, t, :], cq_sorted[b][:, s, t, :], ident_bf16[:])
-            cq_grouped[b] = work.tile([P, HALVES, P, PACK], BF16, name="cq_grouped", align_bytes=64)
-            nc.scalar.copy(out=cq_grouped[b][:], in_=cq_t[:].rearrange("p s t r -> p s r t"))
-
-        def quantise_cq(b):
+        def quantise_cq(b, halves):
             nc.vector.quantize_mx(
-                out=cq_codes[b][:].rearrange("p s r -> p (s r)").bitcast(FP8X4),
-                scales=cq_scales[b][:].rearrange("p s r -> p (s r)"),
-                in_=cq_grouped[b][:].rearrange("p s r t -> p (s r t)"),
+                out=cq_codes[b][:, halves].rearrange("p s r -> p (s r)").bitcast(FP8X4),
+                scales=cq_scales[b][:, halves].rearrange("p s r -> p (s r)"),
+                in_=cq_grouped[b][:, halves].rearrange("p s r t -> p (s r t)"),
             )
 
-        def project_up_and_rotate(b, k):
-            result = results.tile([P, GROUP, HALVES, HEAD], F32, name="result")
-            crossed = swap.tile([P, GROUP, HALVES, ROPE], F32, name="crossed")
-            for s in range(HALVES):
-                rope = psum.tile([P, GROUP, ROPE], F32, name="rope", bufs=3)
-                nope = psum.tile([P, GROUP, NOPE], F32, name="nope", bufs=2)
-                for bank, offset in ((rope, NOPE), (nope, 0)):
-                    for j in range(GROUP):
-                        col = HEAD * j + offset
-                        nc.tensor.matmul_mx(
-                            out=bank[:, j, :],
-                            lhsT=cq_codes[b][:, s, :].bitcast(FP8X4),
-                            lhsT_scale=cq_scales[b][:, s, :],
-                            rhs=wqb_w[:, GROUP_COLS * k + col : GROUP_COLS * k + col + P].bitcast(FP8X4),
-                            rhs_scale=wqb_planes[4 * k : P, col : col + P],
-                            start=True,
-                            stop=True,
-                        )
-                nc.scalar.copy(out=result[:, :, s, 0:NOPE], in_=nope[:])
+        open_results = {}
 
-                nc.vector.tensor_tensor(
-                    out=result[:, :, s, NOPE:HEAD],
-                    in0=rope[:],
-                    in1=cos_pairs[:, s].rearrange("p i e -> p (i e)").unsqueeze(1).to_broadcast([P, GROUP, ROPE]),
-                    op=ALU.mult,
-                )
-                nc.vector.tensor_tensor(
-                    out=crossed[:, :, s, :].rearrange("p h (i e) -> p h i e", e=2),
-                    in0=rope[:].rearrange("p h (i e) -> p h i e", e=2)[:, :, :, ::-1],
-                    in1=sin_pairs[:, s].unsqueeze(1).to_broadcast([P, GROUP, PAIRS, 2]),
-                    op=ALU.mult,
-                )
-                nc.gpsimd.tensor_tensor(
-                    out=result[:, :, s, NOPE:HEAD], in0=result[:, :, s, NOPE:HEAD], in1=crossed[:, :, s, :], op=ALU.add
-                )
-            nc.sync.dma_start(
-                out=out[b, GROUP * k : GROUP * (k + 1)].rearrange("h (p s) f -> p h (s f)", s=HALVES),
-                in_=result[:].rearrange("p h s f -> p h (s f)"),
+        def project_up_and_rotate(b, k, s):
+            if (b, k) not in open_results:
+                open_results[b, k] = [results.tile([P, GROUP, HALVES, HEAD], F32, name="result"), 0]
+            result = open_results[b, k][0]
+            rope = psum.tile([P, GROUP, ROPE], F32, name="rope", bufs=3)
+            nope = psum.tile([P, GROUP, NOPE], F32, name="nope", bufs=2)
+            for bank, offset in ((rope, NOPE), (nope, 0)):
+                for j in range(GROUP):
+                    col = HEAD * j + offset
+                    nc.tensor.matmul_mx(
+                        out=bank[:, j, :],
+                        lhsT=cq_codes[b][:, s, :].bitcast(FP8X4),
+                        lhsT_scale=cq_scales[b][:, s, :],
+                        rhs=wqb_w[:, GROUP_COLS * k + col : GROUP_COLS * k + col + P].bitcast(FP8X4),
+                        rhs_scale=wqb_planes[4 * k : P, col : col + P],
+                        start=True,
+                        stop=True,
+                    )
+            nc.scalar.copy(out=result[:, :, s, 0:NOPE], in_=nope[:])
+
+            crossed = swap.tile([P, GROUP, ROPE], F32, name="crossed")
+            nc.vector.tensor_tensor(
+                out=result[:, :, s, NOPE:HEAD],
+                in0=rope[:],
+                in1=cos_pairs[:, s].rearrange("p i e -> p (i e)").unsqueeze(1).to_broadcast([P, GROUP, ROPE]),
+                op=ALU.mult,
             )
+            nc.vector.tensor_tensor(
+                out=crossed[:].rearrange("p h (i e) -> p h i e", e=2),
+                in0=rope[:].rearrange("p h (i e) -> p h i e", e=2)[:, :, :, ::-1],
+                in1=sin_pairs[:, s].unsqueeze(1).to_broadcast([P, GROUP, PAIRS, 2]),
+                op=ALU.mult,
+            )
+            nc.gpsimd.tensor_tensor(
+                out=result[:, :, s, NOPE:HEAD], in0=result[:, :, s, NOPE:HEAD], in1=crossed[:], op=ALU.add
+            )
+            open_results[b, k][1] += 1
+            if open_results[b, k][1] == HALVES:
+                nc.sync.dma_start(
+                    out=out[b, GROUP * k : GROUP * (k + 1)].rearrange("h (p s) f -> p h (s f)", s=HALVES),
+                    in_=result[:].rearrange("p h s f -> p h (s f)"),
+                )
 
-        transpose_x(0, 0)
-        quantise_x(0, 0)
-        transpose_x(0, 1)
+        both = slice(0, HALVES)
+        transpose_x(0, 0, True)
+        quantise_x(0, slice(0, 1))
         contract_x(0, 0)
-        quantise_x(0, 1)
-        contract_x(0, 1)
-        transpose_cq(0)
-        quantise_cq(0)
+        transpose_x(0, 1, True)
+        quantise_cq(0, slice(0, 1))
+        quantise_x(0, slice(1, 2))
         for b in range(BATCH):
             ahead = b + 1 < BATCH
-            project_up_and_rotate(b, 0)
-            if ahead:
-                transpose_x(b + 1, 0)
-                quantise_x(b + 1, 0)
-            project_up_and_rotate(b, 1)
-            if ahead:
-                contract_x(b + 1, 0)
-                transpose_x(b + 1, 1)
-                quantise_x(b + 1, 1)
-            project_up_and_rotate(b, 2)
-            if ahead:
-                contract_x(b + 1, 1)
-                transpose_cq(b + 1)
-                quantise_cq(b + 1)
-            project_up_and_rotate(b, 3)
+            if b == 0:
+                steps = [(0, 0), (1, 0), (2, 0), (0, 1), (1, 1), (2, 1), (3, 0), (3, 1)]
+                t0_at, t1_at, qx_at, c0_at, c1_at, qc_at = T_AT0
+            else:
+                steps = [(k, s) for k in range(GROUPS) for s in range(HALVES)]
+                t0_at, t1_at, qx_at, c0_at, c1_at, qc_at = T_AT
+            for i, (k, s) in enumerate(steps):
+                if b == 0 and i == 2:
+                    quantise_cq(0, slice(1, 2))
+                if ahead and i == qx_at:
+                    quantise_x(b + 1, both)
+                if ahead and i == qc_at:
+                    quantise_cq(b + 1, both)
+                project_up_and_rotate(b, k, s)
+                if b == 0 and i == 0:
+                    contract_x(0, 1)
+                if ahead and i == t0_at:
+                    transpose_x(b + 1, 0, False)
+                if ahead and i == t1_at:
+                    transpose_x(b + 1, 1, False)
+                if ahead and i == c0_at:
+                    contract_x(b + 1, 0)
+                if ahead and i == c1_at:
+                    contract_x(b + 1, 1)

@@ -222,8 +222,11 @@ def tile_multilatentattention_pa_kernel(tc, x, Wqa_words, Wqa_scales, Wqb_words,
         open_results = {}
 
         def project_up_and_rotate(b, k, s):
+            last = (b, k) == (BATCH - 1, GROUPS - 1)
             if (b, k) not in open_results:
                 open_results[b, k] = [results.tile([P, GROUP, HALVES, HEAD], F32, name="result"), 0]
+                if last:
+                    open_results[b, k].append(keep.tile([P, GROUP, HALVES, ROPE], F32, name="crossed_last"))
             result = open_results[b, k][0]
             rope = psum.tile([P, GROUP, ROPE], F32, name="rope", bufs=3)
             nope = psum.tile([P, GROUP, NOPE], F32, name="nope", bufs=2)
@@ -241,7 +244,11 @@ def tile_multilatentattention_pa_kernel(tc, x, Wqa_words, Wqa_scales, Wqb_words,
                     )
             nc.scalar.copy(out=result[:, :, s, 0:NOPE], in_=nope[:])
 
-            crossed = swap.tile([P, GROUP, ROPE], F32, name="crossed")
+            if last:
+                crossed = open_results[b, k][2][:, :, s, :]
+            else:
+                crossed_tile = swap.tile([P, GROUP, ROPE], F32, name="crossed")
+                crossed = crossed_tile[:]
             nc.vector.tensor_tensor(
                 out=result[:, :, s, NOPE:HEAD],
                 in0=rope[:],
@@ -249,20 +256,38 @@ def tile_multilatentattention_pa_kernel(tc, x, Wqa_words, Wqa_scales, Wqb_words,
                 op=ALU.mult,
             )
             nc.vector.tensor_tensor(
-                out=crossed[:].rearrange("p h (i e) -> p h i e", e=2),
+                out=crossed.rearrange("p h (i e) -> p h i e", e=2),
                 in0=rope[:].rearrange("p h (i e) -> p h i e", e=2)[:, :, :, ::-1],
                 in1=sin_pairs[:, s].unsqueeze(1).to_broadcast([P, GROUP, PAIRS, 2]),
                 op=ALU.mult,
             )
-            nc.gpsimd.tensor_tensor(
-                out=result[:, :, s, NOPE:HEAD], in0=result[:, :, s, NOPE:HEAD], in1=crossed[:], op=ALU.add
-            )
+            return crossed
+
+        def add_and_store(b, k, s, crossed, adder):
+            last = (b, k) == (BATCH - 1, GROUPS - 1)
+            result = open_results[b, k][0]
+            if not last:
+                adder.tensor_tensor(
+                    out=result[:, :, s, NOPE:HEAD], in0=result[:, :, s, NOPE:HEAD], in1=crossed, op=ALU.add
+                )
             open_results[b, k][1] += 1
             if open_results[b, k][1] == HALVES:
-                nc.sync.dma_start(
-                    out=out[b, GROUP * k : GROUP * (k + 1)].rearrange("h (p s) f -> p h (s f)", s=HALVES),
-                    in_=result[:].rearrange("p h s f -> p h (s f)"),
-                )
+                pieces = 2 if last else 1
+                heads = GROUP // pieces
+                for piece in range(pieces):
+                    some = slice(heads * piece, heads * (piece + 1))
+                    if last:
+                        nc.vector.tensor_tensor(
+                            out=result[:, some, :, NOPE:HEAD],
+                            in0=result[:, some, :, NOPE:HEAD],
+                            in1=open_results[b, k][2][:, some],
+                            op=ALU.add,
+                        )
+                    first_head = GROUP * k + heads * piece
+                    nc.sync.dma_start(
+                        out=out[b, first_head : first_head + heads].rearrange("h (p s) f -> p h (s f)", s=HALVES),
+                        in_=result[:, some].rearrange("p h s f -> p h (s f)"),
+                    )
 
         both = slice(0, HALVES)
         transpose_x(0, 0, True)
@@ -279,6 +304,10 @@ def tile_multilatentattention_pa_kernel(tc, x, Wqa_words, Wqa_scales, Wqb_words,
             else:
                 steps = [(k, s) for k in range(GROUPS) for s in range(HALVES)]
                 t0_at, t1_at, qx_at, c0_at, c1_at, qc_at = T_AT
+            quantise_at = [qx_at, qc_at] if ahead else []
+            if b == 0:
+                quantise_at.append(2)
+            waiting = []
             for i, (k, s) in enumerate(steps):
                 if b == 0 and i == 2:
                     quantise_cq(0, slice(1, 2))
@@ -286,7 +315,16 @@ def tile_multilatentattention_pa_kernel(tc, x, Wqa_words, Wqa_scales, Wqb_words,
                     quantise_x(b + 1, both)
                 if ahead and i == qc_at:
                     quantise_cq(b + 1, both)
-                project_up_and_rotate(b, k, s)
+                for held in waiting:
+                    add_and_store(b, held[0], held[1], held[2], nc.vector)
+                waiting.clear()
+                crossed = project_up_and_rotate(b, k, s)
+                if i + 1 in quantise_at:
+                    waiting.append((k, s, crossed))
+                elif (b, k, s) == (BATCH - 1, GROUPS - 2, HALVES - 1):
+                    add_and_store(b, k, s, crossed, nc.vector)
+                else:
+                    add_and_store(b, k, s, crossed, nc.gpsimd)
                 if b == 0 and i == 0:
                     contract_x(0, 1)
                 if ahead and i == t0_at:

@@ -33,8 +33,8 @@ GROUP_COLS = GROUP * HEAD
 FLOPS = 2 * BATCH * POSITIONS * (FEATURES * RANK + RANK * HEADS * HEAD)
 
 
-T_AT0 = (1, 2, 5, 5, 6, 7)
-T_AT = (0, 1, 4, 4, 5, 7)
+T_AT0 = (1, 2, 4, 4, 5, 7)
+T_AT = (0, 1, 3, 3, 4, 6)
 
 
 def build_rotation_tables(nc, pool):

@@ -33,8 +33,7 @@ GROUP_COLS = GROUP * HEAD
 FLOPS = 2 * BATCH * POSITIONS * (FEATURES * RANK + RANK * HEADS * HEAD)
 
 
-T_AT0 = (1, 2, 4, 4, 5, 7)
-T_AT = (0, 1, 3, 3, 4, 6)
+LEAD = 2
 
 
 def build_rotation_tables(nc, pool):
@@ -296,42 +295,34 @@ def tile_multilatentattention_pa_kernel(tc, x, Wqa_words, Wqa_scales, Wqb_words,
         transpose_x(0, 1, True)
         quantise_cq(0, slice(0, 1))
         quantise_x(0, slice(1, 2))
-        for b in range(BATCH):
-            ahead = b + 1 < BATCH
-            if b == 0:
-                steps = [(0, 0), (1, 0), (2, 0), (0, 1), (1, 1), (2, 1), (3, 0), (3, 1)]
-                t0_at, t1_at, qx_at, c0_at, c1_at, qc_at = T_AT0
+        steps = [(0, k, s) for k, s in ((0, 0), (1, 0), (2, 0), (0, 1), (1, 1), (2, 1), (3, 0), (3, 1))]
+        steps += [(b, k, s) for b in range(1, BATCH) for k in range(GROUPS) for s in range(HALVES)]
+        per_batch = GROUPS * HALVES
+
+        in_front = {2: [(quantise_cq, 0, slice(1, 2))]}
+        behind = {0: [(contract_x, 0, 1)]}
+        for b in range(1, BATCH):
+            base = max(1, per_batch * (b - 1) - LEAD)
+            behind.setdefault(base, []).append((transpose_x, b, 0, False))
+            behind.setdefault(base + 1, []).append((transpose_x, b, 1, False))
+            in_front.setdefault(base + 3, []).append((quantise_x, b, both))
+            behind.setdefault(base + 3, []).append((contract_x, b, 0))
+            behind.setdefault(base + 4, []).append((contract_x, b, 1))
+            in_front.setdefault(base + 6, []).append((quantise_cq, b, both))
+
+        waiting = []
+        for n, (b, k, s) in enumerate(steps):
+            for piece in in_front.get(n, []):
+                piece[0](*piece[1:])
+            for held in waiting:
+                add_and_store(held[0], held[1], held[2], held[3], nc.vector)
+            waiting.clear()
+            crossed = project_up_and_rotate(b, k, s)
+            if n + 1 in in_front:
+                waiting.append((b, k, s, crossed))
+            elif (b, k, s) == (BATCH - 1, GROUPS - 2, HALVES - 1):
+                add_and_store(b, k, s, crossed, nc.vector)
             else:
-                steps = [(k, s) for k in range(GROUPS) for s in range(HALVES)]
-                t0_at, t1_at, qx_at, c0_at, c1_at, qc_at = T_AT
-            quantise_at = [qx_at, qc_at] if ahead else []
-            if b == 0:
-                quantise_at.append(2)
-            waiting = []
-            for i, (k, s) in enumerate(steps):
-                if b == 0 and i == 2:
-                    quantise_cq(0, slice(1, 2))
-                if ahead and i == qx_at:
-                    quantise_x(b + 1, both)
-                if ahead and i == qc_at:
-                    quantise_cq(b + 1, both)
-                for held in waiting:
-                    add_and_store(b, held[0], held[1], held[2], nc.vector)
-                waiting.clear()
-                crossed = project_up_and_rotate(b, k, s)
-                if i + 1 in quantise_at:
-                    waiting.append((k, s, crossed))
-                elif (b, k, s) == (BATCH - 1, GROUPS - 2, HALVES - 1):
-                    add_and_store(b, k, s, crossed, nc.vector)
-                else:
-                    add_and_store(b, k, s, crossed, nc.gpsimd)
-                if b == 0 and i == 0:
-                    contract_x(0, 1)
-                if ahead and i == t0_at:
-                    transpose_x(b + 1, 0, False)
-                if ahead and i == t1_at:
-                    transpose_x(b + 1, 1, False)
-                if ahead and i == c0_at:
-                    contract_x(b + 1, 0)
-                if ahead and i == c1_at:
-                    contract_x(b + 1, 1)
+                add_and_store(b, k, s, crossed, nc.gpsimd)
+            for piece in behind.get(n, []):
+                piece[0](*piece[1:])

@@ -143,8 +143,9 @@ def tile_multilatentattention_pa_kernel(tc, x, Wqa_words, Wqa_scales, Wqb_words,
         load_x(0, slice(1, 2))
         load_planes(wqb_planes, Wqb_scales[0].rearrange("r (k c) -> k r c", k=GROUPS))
         load_wqb(0)
+        load_x(1, slice(0, 1))
         load_wqb(1)
-        load_x(1, slice(0, 2))
+        load_x(1, slice(1, 2))
         load_wqb(2)
         load_wqb(3)
         load_x(2, slice(0, 2))
@@ -295,11 +296,11 @@ def tile_multilatentattention_pa_kernel(tc, x, Wqa_words, Wqa_scales, Wqb_words,
         transpose_x(0, 1, True)
         quantise_cq(0, slice(0, 1))
         quantise_x(0, slice(1, 2))
-        steps = [(0, k, s) for k, s in ((0, 0), (1, 0), (2, 0), (0, 1), (1, 1), (2, 1), (3, 0), (3, 1))]
+        steps = [(0, k, s) for s in range(HALVES) for k in range(GROUPS)]
         steps += [(b, k, s) for b in range(1, BATCH) for k in range(GROUPS) for s in range(HALVES)]
         per_batch = GROUPS * HALVES
 
-        in_front = {2: [(quantise_cq, 0, slice(1, 2))]}
+        in_front = {3: [(quantise_cq, 0, slice(1, 2))]}
         behind = {0: [(contract_x, 0, 1)]}
         for b in range(1, BATCH):
             base = max(1, per_batch * (b - 1) - LEAD)

@@ -36,62 +36,44 @@ FLOPS = 2 * BATCH * POSITIONS * (FEATURES * RANK + RANK * HEADS * HEAD)
 LEAD = 2
 
 
-def build_rotation_tables(nc, pool):
+def angle_tables(nc, pool):
     ratio = BASE ** (-2.0 / ROPE)
-    frequency = pool.tile([P, PAIRS], F32, name="frequency")
-    nc.vector.memset(frequency[:, 0:1], 1.0)
+    position = pool.tile([P, HALVES], I32, name="position")
+    nc.gpsimd.iota(position[:], pattern=[[1, HALVES]], base=0, channel_multiplier=HALVES)
+
+    angle = pool.tile([P, HALVES, PAIRS], F32, name="angle")
+    nc.vector.tensor_scalar_mul(out=angle[:, :, 0:1], in0=position[:].unsqueeze(2), scalar1=1.0 / (2.0 * math.pi))
     width = 1
     while width < PAIRS:
-        nc.vector.tensor_scalar_mul(
-            out=frequency[:, width : 2 * width], in0=frequency[:, 0:width], scalar1=ratio**width
-        )
-        width *= 2
+        for m in range(1, 4):
+            nc.vector.tensor_scalar_mul(
+                out=angle[:, :, m * width : (m + 1) * width], in0=angle[:, :, 0:width], scalar1=ratio ** (m * width)
+            )
+        width *= 4
 
-    position_int = pool.tile([P, HALVES], I32, name="position_int")
-    nc.gpsimd.iota(position_int[:], pattern=[[1, HALVES]], base=0, channel_multiplier=HALVES)
-    position = pool.tile([P, HALVES], F32, name="position")
-    nc.vector.tensor_copy(out=position[:], in_=position_int[:])
-
-    turns = pool.tile([P, HALVES, PAIRS], F32, name="turns")
-    for s in range(HALVES):
-        nc.vector.tensor_scalar(
-            out=turns[:, s, :],
-            in0=frequency[:],
-            scalar1=position[:, s : s + 1],
-            scalar2=1.0 / (2.0 * math.pi),
-            op0=ALU.mult,
-            op1=ALU.mult,
-        )
-
-    whole_int = pool.tile([P, HALVES, PAIRS], I32, name="whole_int")
-    nc.vector.tensor_copy(out=whole_int[:], in_=turns[:])
-    whole = pool.tile([P, HALVES, PAIRS], F32, name="whole")
-    nc.vector.tensor_copy(out=whole[:], in_=whole_int[:])
-    part = pool.tile([P, HALVES, PAIRS], F32, name="part")
-    nc.vector.tensor_sub(out=part[:], in0=turns[:], in1=whole[:])
-    part_cos = pool.tile([P, HALVES, PAIRS], F32, name="part_cos")
-    nc.vector.tensor_scalar_add(out=part_cos[:], in0=part[:], scalar1=0.25)
-
-    minus_sin_turns = pool.tile([P, HALVES, PAIRS], F32, name="minus_sin_turns")
+    whole = pool.tile([P, HALVES, PAIRS], I32, name="whole")
+    nc.vector.tensor_copy(out=whole[:], in_=angle[:])
+    part = pool.tile([P, 2, HALVES, PAIRS], F32, name="part")
+    nc.vector.tensor_tensor(out=part[:, 0], in0=angle[:], in1=whole[:], op=ALU.subtract)
+    nc.vector.tensor_scalar_add(out=part[:, 1], in0=part[:, 0], scalar1=0.25)
+    turns = pool.tile([P, 2, HALVES, PAIRS], F32, name="turns")
     nc.vector.scalar_tensor_tensor(
-        out=minus_sin_turns[:], in0=part[:], scalar=0.5, in1=part[:], op0=ALU.is_gt, op1=ALU.subtract
+        out=turns[:], in0=part[:], scalar=0.5, in1=part[:], op0=ALU.is_gt, op1=ALU.subtract
     )
-    minus_cos_turns = pool.tile([P, HALVES, PAIRS], F32, name="minus_cos_turns")
-    nc.vector.scalar_tensor_tensor(
-        out=minus_cos_turns[:], in0=part_cos[:], scalar=0.5, in1=part_cos[:], op0=ALU.is_gt, op1=ALU.subtract
-    )
-
-    sin_pairs = pool.tile([P, HALVES, PAIRS, 2], F32, name="sin_pairs")
-    nc.scalar.activation(out=sin_pairs[:, :, :, 0], in_=minus_sin_turns[:], func=ACT.Sin, scale=2.0 * math.pi)
-    nc.scalar.activation(out=sin_pairs[:, :, :, 1], in_=minus_sin_turns[:], func=ACT.Sin, scale=-2.0 * math.pi)
     cos_pairs = pool.tile([P, HALVES, PAIRS, 2], F32, name="cos_pairs")
+    sin_pairs = pool.tile([P, HALVES, PAIRS, 2], F32, name="sin_pairs")
+    return turns, cos_pairs, sin_pairs
+
+
+def fill_tables(nc, turns, cos_pairs, sin_pairs):
+    nc.scalar.activation(out=sin_pairs[:, :, :, 0], in_=turns[:, 0], func=ACT.Sin, scale=2.0 * math.pi)
+    nc.scalar.activation(out=sin_pairs[:, :, :, 1], in_=turns[:, 0], func=ACT.Sin, scale=-2.0 * math.pi)
     nc.scalar.activation(
         out=cos_pairs[:],
-        in_=minus_cos_turns[:].unsqueeze(3).to_broadcast([P, HALVES, PAIRS, 2]),
+        in_=turns[:, 1].unsqueeze(3).to_broadcast([P, HALVES, PAIRS, 2]),
         func=ACT.Sin,
         scale=-2.0 * math.pi,
     )
-    return cos_pairs, sin_pairs
 
 
 def tile_multilatentattention_pa_kernel(tc, x, Wqa_words, Wqa_scales, Wqb_words, Wqb_scales, out):
@@ -106,8 +88,6 @@ def tile_multilatentattention_pa_kernel(tc, x, Wqa_words, Wqa_scales, Wqb_words,
         wqa_planes_raw = keep.tile([P, RANK], U8, name="wqa_planes_raw", align_bytes=64)
         wqa_planes = keep.tile([P, RANK], U8, name="wqa_planes", align_bytes=64)
         wqb_planes = keep.tile([P, GROUP_COLS], U8, name="wqb_planes", align_bytes=64)
-        nc.vector.memset(wqa_planes_raw[:].bitcast(I32), 0)
-        nc.vector.memset(wqb_planes[:].bitcast(I32), 0)
 
         x_sb = [keep.tile([P, HALVES, FEATURES], BF16, name="x%d" % b) for b in range(BATCH)]
         wqa_raw = keep.tile([P, X_PASSES, RANK], I32, name="wqa_raw", align_bytes=64)
@@ -136,30 +116,8 @@ def tile_multilatentattention_pa_kernel(tc, x, Wqa_words, Wqa_scales, Wqb_words,
             cols = slice(GROUP_COLS * k, GROUP_COLS * (k + 1))
             nc.sync.dma_start(out=wqb_w[:, cols].bitcast(I32), in_=wqb_dram[:, cols])
 
-        load_x(0, slice(0, 1))
-        load_planes(wqa_planes_raw, Wqa_scales)
-        load_wqa(slice(0, 2))
-        load_wqa(slice(2, 4))
-        load_x(0, slice(1, 2))
-        load_planes(wqb_planes, Wqb_scales[0].rearrange("r (k c) -> k r c", k=GROUPS))
-        load_wqb(0)
-        load_x(1, slice(0, 1))
-        load_wqb(1)
-        load_x(1, slice(1, 2))
-        load_wqb(2)
-        load_wqb(3)
-        load_x(2, slice(0, 2))
-        load_x(3, slice(0, 2))
 
-        ident_f32 = keep.tile([P, P], F32, name="ident_f32")
-        make_identity(nc, ident_f32[:])
-        cos_pairs, sin_pairs = build_rotation_tables(nc, keep)
-
-        nc.gpsimd.tensor_copy(
-            out=wqa_planes[:].rearrange("p (t m) -> p m t", t=PACK),
-            in_=wqa_planes_raw[:].rearrange("p (m t) -> p m t", t=PACK),
-        )
-        for g in range(X_PASSES):
+        def sort_wqa(g):
             nc.vector.tensor_copy(out=wqa_w[:, g], in_=wqa_raw[:, g, :].rearrange("p (m t) -> p t m", t=PACK))
 
         x_grouped = [None] * BATCH
@@ -169,12 +127,12 @@ def tile_multilatentattention_pa_kernel(tc, x, Wqa_words, Wqa_scales, Wqb_words,
         cq_codes = [keep.tile([P, HALVES, P], U32, name="cq_codes%d" % b, align_bytes=64) for b in range(BATCH)]
         cq_scales = [keep.tile([P, HALVES, P], U8, name="cq_scales%d" % b, align_bytes=64) for b in range(BATCH)]
 
-        def transpose_x(b, s, helper):
+        def transpose_x(b, s, halves=range(2)):
             x_pairs = x_sb[b][:, s, :].bitcast(F32)
-            if s == 0:
+            if s == 0 and halves[0] == 0:
                 x_grouped[b] = work.tile([P, HALVES, FEATURES], BF16, name="x_grouped", align_bytes=64)
             grouped_pairs = x_grouped[b][:, s, :].bitcast(F32).rearrange("p (g r u) -> p g r u", g=X_PASSES, u=2)
-            for half in range(2):
+            for half in halves:
                 x_t = psum.tile([P, 2, 2, P], F32, name="x_t", bufs=2)
                 for i in range(2):
                     first = (K_PASS // 2) * (2 * half + i)
@@ -182,8 +140,7 @@ def tile_multilatentattention_pa_kernel(tc, x, Wqa_words, Wqa_scales, Wqb_words,
                         nc.tensor.transpose(
                             x_t[:, i, u, :], x_pairs[:, first + u : first + K_PASS // 2 : 2], ident_f32[:]
                         )
-                copy = nc.vector.tensor_copy if (helper and half == 1) else nc.scalar.copy
-                copy(out=grouped_pairs[:, 2 * half : 2 * half + 2], in_=x_t[:].rearrange("p g u r -> p g r u"))
+                nc.scalar.copy(out=grouped_pairs[:, 2 * half : 2 * half + 2], in_=x_t[:].rearrange("p g u r -> p g r u"))
 
         def quantise_x(b, halves):
             if halves.start == 0:
@@ -290,12 +247,55 @@ def tile_multilatentattention_pa_kernel(tc, x, Wqa_words, Wqa_scales, Wqb_words,
                     )
 
         both = slice(0, HALVES)
-        transpose_x(0, 0, True)
-        quantise_x(0, slice(0, 1))
-        contract_x(0, 0)
-        transpose_x(0, 1, True)
-        quantise_cq(0, slice(0, 1))
-        quantise_x(0, slice(1, 2))
+        with tc.manual_schedule():
+            one_zero = keep.tile([P, 1], F32, name="one_zero")
+            nc.vector.memset(one_zero[:], 0.0)
+            one_sine = keep.tile([P, 1], F32, name="one_sine")
+            nc.scalar.activation(out=one_sine[:], in_=one_zero[:], func=ACT.Sin)
+
+            nc.vector.memset(wqa_planes_raw[:].bitcast(I32), 0)
+            nc.vector.memset(wqb_planes[:].bitcast(I32), 0)
+
+            load_x(0, slice(0, 1))
+            load_planes(wqa_planes_raw, Wqa_scales)
+            load_wqa(slice(0, 2))
+            load_wqa(slice(2, 4))
+            load_x(0, slice(1, 2))
+            load_planes(wqb_planes, Wqb_scales[0].rearrange("r (k c) -> k r c", k=GROUPS))
+            load_wqb(0)
+            load_x(1, slice(0, 1))
+            load_wqb(1)
+            load_x(1, slice(1, 2))
+            load_wqb(2)
+            load_wqb(3)
+            load_x(2, slice(0, 2))
+            load_x(3, slice(0, 2))
+
+            turns, cos_pairs, sin_pairs = angle_tables(nc, keep)
+            ident_f32 = keep.tile([P, P], F32, name="ident_f32")
+            make_identity(nc, ident_f32[:])
+
+            nc.gpsimd.tensor_copy(
+                out=wqa_planes[:].rearrange("p (t m) -> p m t", t=PACK),
+                in_=wqa_planes_raw[:].rearrange("p (m t) -> p m t", t=PACK),
+            )
+
+            transpose_x(0, 0)
+            heat = psum.tile([P, 512], F32, name="heat", tag="nope", bufs=2)
+            for turn in range(4):
+                nc.tensor.matmul(heat[:], lhsT=x_sb[0][:, 0, 0:P], rhs=x_sb[0][:, 0, 0:512], start=True, stop=True)
+            sort_wqa(0)
+            sort_wqa(1)
+            quantise_x(0, slice(0, 1))
+            sort_wqa(2)
+            sort_wqa(3)
+            fill_tables(nc, turns, cos_pairs, sin_pairs)
+            transpose_x(0, 1, range(0, 1))
+            contract_x(0, 0)
+            transpose_x(0, 1, range(1, 2))
+            quantise_cq(0, slice(0, 1))
+            quantise_x(0, slice(1, 2))
+
         steps = [(0, k, s) for s in range(HALVES) for k in range(GROUPS)]
         steps += [(b, k, s) for b in range(1, BATCH) for k in range(GROUPS) for s in range(HALVES)]
         per_batch = GROUPS * HALVES
@@ -304,8 +304,8 @@ def tile_multilatentattention_pa_kernel(tc, x, Wqa_words, Wqa_scales, Wqb_words,
         behind = {0: [(contract_x, 0, 1)]}
         for b in range(1, BATCH):
             base = max(1, per_batch * (b - 1) - LEAD)
-            behind.setdefault(base, []).append((transpose_x, b, 0, False))
-            behind.setdefault(base + 1, []).append((transpose_x, b, 1, False))
+            behind.setdefault(base, []).append((transpose_x, b, 0))
+            behind.setdefault(base + 1, []).append((transpose_x, b, 1))
             in_front.setdefault(base + 3, []).append((quantise_x, b, both))
             behind.setdefault(base + 3, []).append((contract_x, b, 0))
             behind.setdefault(base + 4, []).append((contract_x, b, 1))

@@ -306,6 +306,14 @@ def tile_multilatentattention_pa_kernel(tc, x, Wqa_words, Wqa_scales, Wqb_words,
             base = max(1, per_batch * (b - 1) - LEAD)
             behind.setdefault(base, []).append((transpose_x, b, 0))
             behind.setdefault(base + 1, []).append((transpose_x, b, 1))
+            if b == 1:
+                in_front.setdefault(base + 2, []).append((quantise_x, b, slice(0, 1)))
+                behind.setdefault(base + 2, []).append((contract_x, b, 0))
+                in_front.setdefault(base + 3, []).append((quantise_x, b, slice(1, 2)))
+                behind.setdefault(base + 3, []).append((contract_x, b, 1))
+                in_front.setdefault(base + 4, []).append((quantise_cq, b, slice(0, 1)))
+                in_front.setdefault(base + 5, []).append((quantise_cq, b, slice(1, 2)))
+                continue
             in_front.setdefault(base + 3, []).append((quantise_x, b, both))
             behind.setdefault(base + 3, []).append((contract_x, b, 0))
             behind.setdefault(base + 4, []).append((contract_x, b, 1))
@@ -319,7 +327,7 @@ def tile_multilatentattention_pa_kernel(tc, x, Wqa_words, Wqa_scales, Wqb_words,
                 add_and_store(held[0], held[1], held[2], held[3], nc.vector)
             waiting.clear()
             crossed = project_up_and_rotate(b, k, s)
-            if n + 1 in in_front:
+            if any(piece[0] is quantise_x for piece in in_front.get(n + 1, [])):
                 waiting.append((b, k, s, crossed))
             elif (b, k, s) == (BATCH - 1, GROUPS - 2, HALVES - 1):
                 add_and_store(b, k, s, crossed, nc.vector)

import math
from contextlib import ExitStack

import concourse.mybir as mybir
from concourse.masks import make_identity

F32 = mybir.dt.float32
BF16 = mybir.dt.bfloat16
I32 = mybir.dt.int32
U32 = mybir.dt.uint32
U8 = mybir.dt.uint8
FP8X4 = mybir.dt.float8_e4m3fn_x4
ALU = mybir.AluOpType
ACT = mybir.ActivationFunctionType

P = 128
PACK = 4
K_PASS = P * PACK

BATCH, POSITIONS, FEATURES = 4, 256, 2048
RANK = 512
HEADS, NOPE, ROPE = 16, 128, 128
HEAD = NOPE + ROPE
PAIRS = ROPE // 2
BASE = 10000.0

HALVES = POSITIONS // P
X_PASSES = FEATURES // K_PASS
GROUP = 4
GROUPS = HEADS // GROUP
GROUP_COLS = GROUP * HEAD

FLOPS = 2 * BATCH * POSITIONS * (FEATURES * RANK + RANK * HEADS * HEAD)


LEAD = 2


def angle_tables(nc, pool):
    ratio = BASE ** (-2.0 / ROPE)
    position = pool.tile([P, HALVES], I32, name="position")
    nc.gpsimd.iota(position[:], pattern=[[1, HALVES]], base=0, channel_multiplier=HALVES)

    angle = pool.tile([P, HALVES, PAIRS], F32, name="angle")
    nc.vector.tensor_scalar_mul(out=angle[:, :, 0:1], in0=position[:].unsqueeze(2), scalar1=1.0 / (2.0 * math.pi))
    width = 1
    while width < PAIRS:
        for m in range(1, 4):
            nc.vector.tensor_scalar_mul(
                out=angle[:, :, m * width : (m + 1) * width], in0=angle[:, :, 0:width], scalar1=ratio ** (m * width)
            )
        width *= 4

    whole = pool.tile([P, HALVES, PAIRS], I32, name="whole")
    nc.vector.tensor_copy(out=whole[:], in_=angle[:])
    part = pool.tile([P, 2, HALVES, PAIRS], F32, name="part")
    nc.vector.tensor_tensor(out=part[:, 0], in0=angle[:], in1=whole[:], op=ALU.subtract)
    nc.vector.tensor_scalar_add(out=part[:, 1], in0=part[:, 0], scalar1=0.25)
    turns = pool.tile([P, 2, HALVES, PAIRS], F32, name="turns")
    nc.vector.scalar_tensor_tensor(
        out=turns[:], in0=part[:], scalar=0.5, in1=part[:], op0=ALU.is_gt, op1=ALU.subtract
    )
    cos_pairs = pool.tile([P, HALVES, PAIRS, 2], F32, name="cos_pairs")
    sin_pairs = pool.tile([P, HALVES, PAIRS, 2], F32, name="sin_pairs")
    return turns, cos_pairs, sin_pairs


def fill_tables(nc, turns, cos_pairs, sin_pairs):
    nc.scalar.activation(out=sin_pairs[:, :, :, 0], in_=turns[:, 0], func=ACT.Sin, scale=2.0 * math.pi)
    nc.scalar.activation(out=sin_pairs[:, :, :, 1], in_=turns[:, 0], func=ACT.Sin, scale=-2.0 * math.pi)
    nc.scalar.activation(
        out=cos_pairs[:],
        in_=turns[:, 1].unsqueeze(3).to_broadcast([P, HALVES, PAIRS, 2]),
        func=ACT.Sin,
        scale=-2.0 * math.pi,
    )


def tile_multilatentattention_pa_kernel(tc, x, Wqa_words, Wqa_scales, Wqb_words, Wqb_scales, out):
    nc = tc.nc
    with ExitStack() as ctx:
        keep = ctx.enter_context(tc.tile_pool(name="keep", bufs=1))
        work = ctx.enter_context(tc.tile_pool(name="work", bufs=2))
        swap = ctx.enter_context(tc.tile_pool(name="swap", bufs=4))
        results = ctx.enter_context(tc.tile_pool(name="results", bufs=6))
        psum = ctx.enter_context(tc.psum_pool(name="psum", bufs=1))

        wqa_planes_raw = keep.tile([P, RANK], U8, name="wqa_planes_raw", align_bytes=64)
        wqa_planes = keep.tile([P, RANK], U8, name="wqa_planes", align_bytes=64)
        wqb_planes = keep.tile([P, GROUP_COLS], U8, name="wqb_planes", align_bytes=64)

        x_sb = [keep.tile([P, HALVES, FEATURES], BF16, name="x%d" % b) for b in range(BATCH)]
        wqa_raw = keep.tile([P, X_PASSES, RANK], I32, name="wqa_raw", align_bytes=64)
        wqa_w = keep.tile([P, X_PASSES, PACK, P], I32, name="wqa_w", align_bytes=64)
        wqb_w = keep.tile([P, HEADS * HEAD], U32, name="wqb_w", align_bytes=64)
        wqb_dram = Wqb_words.rearrange("g p n t -> p (g n t)").bitcast(I32)

        def load_x(b, halves):
            nc.sync.dma_start(
                out=x_sb[b][:, halves, :], in_=x[b].rearrange("(p s) e -> p s e", s=HALVES)[:, halves, :]
            )

        def load_planes(planes, scale_rows):
            for quadrant in range(4):
                nc.sync.dma_start(
                    out=planes[32 * quadrant : 32 * quadrant + 16, :].bitcast(I32),
                    in_=scale_rows[:, 4 * quadrant : 4 * quadrant + 4, :].bitcast(I32),
                )

        def load_wqa(passes):
            nc.sync.dma_start(
                out=wqa_raw[:, passes, :], in_=Wqa_words.rearrange("g p n t -> p g (n t)").bitcast(I32)[:, passes, :]
            )

        def load_wqb(k):
            cols = slice(GROUP_COLS * k, GROUP_COLS * (k + 1))
            nc.sync.dma_start(out=wqb_w[:, cols].bitcast(I32), in_=wqb_dram[:, cols])


        def sort_wqa(g):
            nc.vector.tensor_copy(out=wqa_w[:, g], in_=wqa_raw[:, g, :].rearrange("p (m t) -> p t m", t=PACK))

        x_grouped = [None] * BATCH
        x_codes = [None] * BATCH
        x_scales = [None] * BATCH
        cq_grouped = [None] * BATCH
        cq_codes = [keep.tile([P, HALVES, P], U32, name="cq_codes%d" % b, align_bytes=64) for b in range(BATCH)]
        cq_scales = [keep.tile([P, HALVES, P], U8, name="cq_scales%d" % b, align_bytes=64) for b in range(BATCH)]

        def transpose_x(b, s, halves=range(2)):
            x_pairs = x_sb[b][:, s, :].bitcast(F32)
            if s == 0 and halves[0] == 0:
                x_grouped[b] = work.tile([P, HALVES, FEATURES], BF16, name="x_grouped", align_bytes=64)
            grouped_pairs = x_grouped[b][:, s, :].bitcast(F32).rearrange("p (g r u) -> p g r u", g=X_PASSES, u=2)
            for half in halves:
                x_t = psum.tile([P, 2, 2, P], F32, name="x_t", bufs=2)
                for i in range(2):
                    first = (K_PASS // 2) * (2 * half + i)
                    for u in range(2):
                        nc.tensor.transpose(
                            x_t[:, i, u, :], x_pairs[:, first + u : first + K_PASS // 2 : 2], ident_f32[:]
                        )
                nc.scalar.copy(out=grouped_pairs[:, 2 * half : 2 * half + 2], in_=x_t[:].rearrange("p g u r -> p g r u"))

        def quantise_x(b, halves):
            if halves.start == 0:
                x_codes[b] = work.tile([P, HALVES, X_PASSES, P], U32, name="x_codes", align_bytes=64)
                x_scales[b] = work.tile([P, HALVES, X_PASSES, P], U8, name="x_scales", align_bytes=64)
            nc.vector.quantize_mx(
                out=x_codes[b][:, halves].rearrange("p s g r -> p (s g r)").bitcast(FP8X4),
                scales=x_scales[b][:, halves].rearrange("p s g r -> p (s g r)"),
                in_=x_grouped[b][:, halves].rearrange("p s e -> p (s e)"),
            )

        def contract_x(b, s):
            cq_t = psum.tile([P, PACK, P], F32, name="cq_t", tag="cq")
            for t in range(PACK):
                for g in range(X_PASSES):
                    nc.tensor.matmul_mx(
                        out=cq_t[:, t, :],
                        lhsT=wqa_w[:, g, t, :].bitcast(FP8X4),
                        lhsT_scale=wqa_planes[4 * g : P, P * t : P * (t + 1)],
                        rhs=x_codes[b][:, s, g, :].bitcast(FP8X4),
                        rhs_scale=x_scales[b][:, s, g, :],
                        start=(g == 0),
                        stop=(g == X_PASSES - 1),
                    )
            if s == 0:
                cq_grouped[b] = work.tile([P, HALVES, P, PACK], BF16, name="cq_grouped", align_bytes=64)
            nc.scalar.copy(out=cq_grouped[b][:, s], in_=cq_t[:].rearrange("p t r -> p r t"))

        def quantise_cq(b, halves):
            nc.vector.quantize_mx(
                out=cq_codes[b][:, halves].rearrange("p s r -> p (s r)").bitcast(FP8X4),
                scales=cq_scales[b][:, halves].rearrange("p s r -> p (s r)"),
                in_=cq_grouped[b][:, halves].rearrange("p s r t -> p (s r t)"),
            )

        open_results = {}

        def project_up_and_rotate(b, k, s):
            last = (b, k) == (BATCH - 1, GROUPS - 1)
            if (b, k) not in open_results:
                open_results[b, k] = [results.tile([P, GROUP, HALVES, HEAD], F32, name="result"), 0]
                if last:
                    open_results[b, k].append(keep.tile([P, GROUP, HALVES, ROPE], F32, name="crossed_last"))
            result = open_results[b, k][0]
            rope = psum.tile([P, GROUP, ROPE], F32, name="rope", bufs=3)
            nope = psum.tile([P, GROUP, NOPE], F32, name="nope", bufs=2)
            for bank, offset in ((rope, NOPE), (nope, 0)):
                for j in range(GROUP):
                    col = HEAD * j + offset
                    nc.tensor.matmul_mx(
                        out=bank[:, j, :],
                        lhsT=cq_codes[b][:, s, :].bitcast(FP8X4),
                        lhsT_scale=cq_scales[b][:, s, :],
                        rhs=wqb_w[:, GROUP_COLS * k + col : GROUP_COLS * k + col + P].bitcast(FP8X4),
                        rhs_scale=wqb_planes[4 * k : P, col : col + P],
                        start=True,
                        stop=True,
                    )
            nc.scalar.copy(out=result[:, :, s, 0:NOPE], in_=nope[:])

            if last:
                crossed = open_results[b, k][2][:, :, s, :]
            else:
                crossed_tile = swap.tile([P, GROUP, ROPE], F32, name="crossed")
                crossed = crossed_tile[:]
            nc.vector.tensor_tensor(
                out=result[:, :, s, NOPE:HEAD],
                in0=rope[:],
                in1=cos_pairs[:, s].rearrange("p i e -> p (i e)").unsqueeze(1).to_broadcast([P, GROUP, ROPE]),
                op=ALU.mult,
            )
            nc.vector.tensor_tensor(
                out=crossed.rearrange("p h (i e) -> p h i e", e=2),
                in0=rope[:].rearrange("p h (i e) -> p h i e", e=2)[:, :, :, ::-1],
                in1=sin_pairs[:, s].unsqueeze(1).to_broadcast([P, GROUP, PAIRS, 2]),
                op=ALU.mult,
            )
            return crossed

        def add_and_store(b, k, s, crossed, adder):
            last = (b, k) == (BATCH - 1, GROUPS - 1)
            result = open_results[b, k][0]
            if not last:
                adder.tensor_tensor(
                    out=result[:, :, s, NOPE:HEAD], in0=result[:, :, s, NOPE:HEAD], in1=crossed, op=ALU.add
                )
            open_results[b, k][1] += 1
            if open_results[b, k][1] == HALVES:
                pieces = 2 if last else 1
                heads = GROUP // pieces
                for piece in range(pieces):
                    some = slice(heads * piece, heads * (piece + 1))
                    if last:
                        nc.vector.tensor_tensor(
                            out=result[:, some, :, NOPE:HEAD],
                            in0=result[:, some, :, NOPE:HEAD],
                            in1=open_results[b, k][2][:, some],
                            op=ALU.add,
                        )
                    first_head = GROUP * k + heads * piece
                    nc.sync.dma_start(
                        out=out[b, first_head : first_head + heads].rearrange("h (p s) f -> p h (s f)", s=HALVES),
                        in_=result[:, some].rearrange("p h s f -> p h (s f)"),
                    )

        both = slice(0, HALVES)
        with tc.manual_schedule():
            one_zero = keep.tile([P, 1], F32, name="one_zero")
            nc.vector.memset(one_zero[:], 0.0)
            one_sine = keep.tile([P, 1], F32, name="one_sine")
            nc.scalar.activation(out=one_sine[:], in_=one_zero[:], func=ACT.Sin)

            nc.vector.memset(wqa_planes_raw[:].bitcast(I32), 0)
            nc.vector.memset(wqb_planes[:].bitcast(I32), 0)

            load_x(0, slice(0, 1))
            load_planes(wqa_planes_raw, Wqa_scales)
            load_wqa(slice(0, 2))
            load_wqa(slice(2, 4))
            load_x(0, slice(1, 2))
            load_planes(wqb_planes, Wqb_scales[0].rearrange("r (k c) -> k r c", k=GROUPS))
            load_wqb(0)
            load_x(1, slice(0, 1))
            load_wqb(1)
            load_x(1, slice(1, 2))
            load_wqb(2)
            load_wqb(3)
            load_x(2, slice(0, 2))
            load_x(3, slice(0, 2))

            turns, cos_pairs, sin_pairs = angle_tables(nc, keep)
            ident_f32 = keep.tile([P, P], F32, name="ident_f32")
            make_identity(nc, ident_f32[:])

            nc.gpsimd.tensor_copy(
                out=wqa_planes[:].rearrange("p (t m) -> p m t", t=PACK),
                in_=wqa_planes_raw[:].rearrange("p (m t) -> p m t", t=PACK),
            )

            transpose_x(0, 0)
            heat = psum.tile([P, 512], F32, name="heat", tag="nope", bufs=2)
            for turn in range(4):
                nc.tensor.matmul(heat[:], lhsT=x_sb[0][:, 0, 0:P], rhs=x_sb[0][:, 0, 0:512], start=True, stop=True)
            sort_wqa(0)
            sort_wqa(1)
            quantise_x(0, slice(0, 1))
            sort_wqa(2)
            sort_wqa(3)
            fill_tables(nc, turns, cos_pairs, sin_pairs)
            transpose_x(0, 1, range(0, 1))
            contract_x(0, 0)
            transpose_x(0, 1, range(1, 2))
            quantise_cq(0, slice(0, 1))
            quantise_x(0, slice(1, 2))

        steps = [(0, k, s) for s in range(HALVES) for k in range(GROUPS)]
        steps += [(b, k, s) for b in range(1, BATCH) for k in range(GROUPS) for s in range(HALVES)]
        per_batch = GROUPS * HALVES

        in_front = {3: [(quantise_cq, 0, slice(1, 2))]}
        behind = {0: [(contract_x, 0, 1)]}
        for b in range(1, BATCH):
            base = max(1, per_batch * (b - 1) - LEAD)
            behind.setdefault(base, []).append((transpose_x, b, 0))
            behind.setdefault(base + 1, []).append((transpose_x, b, 1))
            if b == 1:
                in_front.setdefault(base + 2, []).append((quantise_x, b, slice(0, 1)))
                behind.setdefault(base + 2, []).append((contract_x, b, 0))
                in_front.setdefault(base + 3, []).append((quantise_x, b, slice(1, 2)))
                behind.setdefault(base + 3, []).append((contract_x, b, 1))
                in_front.setdefault(base + 4, []).append((quantise_cq, b, slice(0, 1)))
                in_front.setdefault(base + 5, []).append((quantise_cq, b, slice(1, 2)))
                continue
            in_front.setdefault(base + 3, []).append((quantise_x, b, both))
            behind.setdefault(base + 3, []).append((contract_x, b, 0))
            behind.setdefault(base + 4, []).append((contract_x, b, 1))
            in_front.setdefault(base + 6, []).append((quantise_cq, b, both))

        waiting = []
        for n, (b, k, s) in enumerate(steps):
            for piece in in_front.get(n, []):
                piece[0](*piece[1:])
            for held in waiting:
                add_and_store(held[0], held[1], held[2], held[3], nc.vector)
            waiting.clear()
            crossed = project_up_and_rotate(b, k, s)
            if any(piece[0] is quantise_x for piece in in_front.get(n + 1, [])):
                waiting.append((b, k, s, crossed))
            elif (b, k, s) == (BATCH - 1, GROUPS - 2, HALVES - 1):
                add_and_store(b, k, s, crossed, nc.vector)
            else:
                add_and_store(b, k, s, crossed, nc.gpsimd)
            for piece in behind.get(n, []):
                piece[0](*piece[1:])
